import numpy as np
import ml_dtypes


def mxq(x, axis, fmt="e4m3"):
    dtype, down = {"e4m3": (ml_dtypes.float8_e4m3fn, 7), "e5m2": (ml_dtypes.float8_e5m2, 14)}[fmt]
    v = np.moveaxis(np.asarray(x, np.float32).astype(ml_dtypes.bfloat16).astype(np.float64), axis, -1)
    blocks = v.reshape(v.shape[:-1] + (-1, 32))
    amax = np.abs(blocks).max(-1, keepdims=True)
    byte = np.maximum(np.where(amax > 0, np.frexp(amax)[1] - 1 + 127, 0) - down, 1)
    scale = np.exp2(byte - 127.0)
    codes = (blocks / scale).astype(np.float32).astype(dtype).astype(np.float64)
    return np.moveaxis((codes * scale).reshape(v.shape), -1, axis)


WIDE = False


def mx_kscale(k):
    if not WIDE:
        return np.ones(k)
    levels = np.array([10, -10, 5, -5, 0])
    if k % 512:
        return np.exp2(np.random.permutation(np.resize(levels, k // 32))).repeat(32)
    a = np.empty((k // 512, 16))
    for p in range(k // 512):
        a[p, :8] = np.random.permutation(np.resize(levels, 8))
        for g in range(8):
            far = levels[np.abs(levels - a[p, g]) >= 10]
            a[p, g + 8] = far[np.random.randint(len(far))]
    return np.exp2(a.ravel()).repeat(32)


BF16 = ml_dtypes.bfloat16


def bf(x):
    return np.asarray(x, np.float32).astype(BF16)


def f64(x):
    return np.asarray(x).astype(np.float64)


B, S, E, H, DH, L = 2, 512, 2048, 16, 128, 512
NOPE = DH // 4
ROPE_D = DH - NOPE
THETA = 10000.0


def rope_tables(seq_len):
    freqs = 1.0 / THETA ** (np.arange(0, ROPE_D, 2) / ROPE_D)
    emb = np.arange(seq_len)[:, None] * freqs[None, :]
    return np.cos(emb), np.sin(emb)


def apply_rope(x, cos, sin):
    xe, xo = x[..., ::2], x[..., 1::2]
    return np.concatenate([xe * cos - xo * sin, xo * cos + xe * sin], axis=-1)


def setup_inputs():
    s = mx_kscale(E)
    return {"x": bf(np.random.standard_normal((B, S, E)) * s),
            "Wq": bf(np.random.standard_normal((E, H * DH)) / np.sqrt(E) / s[:, None])}


def core(x, Wq):
    q = (mxq(f64(x), 2, "e4m3") @ mxq(f64(Wq), 0, "e4m3")).reshape(B, S, H, DH).transpose(0, 2, 1, 3)
    q_nope, q_rope = q[..., :NOPE], q[..., NOPE:]
    cos, sin = rope_tables(S)
    q_rope = apply_rope(q_rope, cos, sin)
    return np.concatenate([q_nope, q_rope], axis=-1)


def e4m3fn_bytes(y):
    return np.clip(np.asarray(y, np.float64), -448.0, 448.0).astype(np.float32).astype(ml_dtypes.float8_e4m3fn).view(np.uint8)


def reference(x, Wq):
    out = core(x, Wq)
    s = np.max(np.abs(out), axis=-1, keepdims=True) / 448.0
    return out, e4m3fn_bytes(out / s)

@@ -1,0 +1,568 @@
+from contextlib import ExitStack
+
+import concourse.mybir as mybir
+from concourse.masks import make_identity
+
+F32 = mybir.dt.float32
+BF16 = mybir.dt.bfloat16
+U32 = mybir.dt.uint32
+U8 = mybir.dt.uint8
+I32 = mybir.dt.int32
+FP8 = mybir.dt.float8_e4m3fn
+FP8X4 = mybir.dt.float8_e4m3fn_x4
+ALU = mybir.AluOpType
+ACT = mybir.ActivationFunctionType
+AX = mybir.AxisListType
+
+FLOPS = 2 * 1024 * 2048 * 2048
+
+P = 128
+NB, NI, NG, NH = 2, 4, 4, 16
+D, NOPE, HALF = 128, 32, 48
+ROPE = 2 * HALF
+W_CHUNKS = ((0, 256), (256, 256), (512, 512), (1024, 512), (1536, 512))
+TWO_PI = 6.283185307179586
+RHO = 10000.0 ** (-1.0 / 48.0)
+NACC = 6
+GROPE = (21, 25, 29)
+
+
+def tile_mla_pb_kernel(tc, x, Wq, out_0, out_1):
+    nc = tc.nc
+    with ExitStack() as ctx:
+        pool = ctx.enter_context(tc.tile_pool(name="sb", bufs=1))
+        psum = ctx.enter_context(tc.psum_pool(name="ps", bufs=1))
+
+        x_codes = pool.tile([P, NB, NI, NG * P], U32, name="x_codes", align_bytes=64)
+        x_scales = pool.tile([P, NB, NI, NG * P], U8, name="x_scales", align_bytes=64)
+        ws_codes = pool.tile([P, 2, NG, 256], U32, name="ws_codes", align_bytes=64)
+        ws_scales = pool.tile([P, 2, NG, 256], U8, name="ws_scales", align_bytes=64)
+        wb_codes = pool.tile([P, 3, NG, 512], U32, name="wb_codes", align_bytes=64)
+        wb_scales = pool.tile([P, 3, NG, 512], U8, name="wb_scales", align_bytes=64)
+
+        x_raw = {}
+        w_raw = {}
+
+        def load_x(b, i):
+            t = pool.tile([P, 2048], BF16, name="x_raw%d" % i)
+            nc.sync.dma_start(out=t[:], in_=x[b].rearrange("(p i) k -> p i k", i=NI)[:, i, :])
+            x_raw[(b, i)] = t
+
+        def load_w(c, g):
+            c0, width = W_CHUNKS[c]
+            t = pool.tile([P, 4, width], BF16, name="w_raw%d_%d" % (2 if c == 4 else c, g))
+            nc.sync.dma_start(out=t[:], in_=Wq[512 * g:512 * (g + 1), c0:c0 + width].rearrange("(p j) w -> p j w", j=4))
+            w_raw[(c, g)] = t
+
+        load_x(0, 0)
+        load_x(0, 1)
+        for g in range(NG):
+            load_w(0, g)
+        load_x(0, 2)
+        load_x(0, 3)
+        for g in range(NG):
+            load_w(1, g)
+
+        warm = pool.tile([P, 1], F32, name="warm")
+        nc.vector.memset(warm[:], 0.0)
+        nc.scalar.activation(out=warm[:], in_=warm[:], func=ACT.Sin)
+        pos_i = pool.tile([P, NI], I32, name="pos_i")
+        nc.gpsimd.iota(pos_i[:], pattern=[[1, NI]], base=0, channel_multiplier=NI)
+        ident = pool.tile([P, P], F32, name="ident")
+        make_identity(nc, ident[:])
+        zero = pool.tile([P, 1], F32, name="zero")
+        nc.vector.memset(zero[:], 0.0)
+        pos_f = pool.tile([P, NI], F32, name="pos_f")
+        nc.vector.tensor_copy(out=pos_f[:], in_=pos_i[:])
+        turns = pool.tile([P, 2, NI, HALF], F32, name="turns")
+        nc.vector.tensor_scalar(out=turns[:, 0, :, 0:1], in0=pos_f[:].unsqueeze(2), scalar1=1.0 / TWO_PI, scalar2=None,
+                                op0=ALU.mult)
+        for w in (1, 2, 4, 8, 16, 32):
+            n = min(w, HALF - w)
+            nc.vector.tensor_scalar(out=turns[:, 0, :, w:w + n], in0=turns[:, 0, :, 0:n], scalar1=RHO ** w, scalar2=None,
+                                    op0=ALU.mult)
+        nc.vector.tensor_scalar(out=turns[:, 1], in0=turns[:, 0], scalar1=0.25, scalar2=None, op0=ALU.add)
+        whole_i = pool.tile([P, 2, NI, HALF], I32, name="whole_i")
+        nc.vector.tensor_copy(out=whole_i[:], in_=turns[:])
+        whole_f = pool.tile([P, 2, NI, HALF], F32, name="whole_f")
+        nc.vector.tensor_copy(out=whole_f[:], in_=whole_i[:])
+        frac = pool.tile([P, 2, NI, HALF], F32, name="frac")
+        nc.vector.tensor_tensor(out=frac[:], in0=turns[:], in1=whole_f[:], op=ALU.subtract)
+        nfrac = pool.tile([P, 2, NI, HALF], F32, name="nfrac")
+        fl = "p k i j -> p (k i j)"
+        nc.vector.scalar_tensor_tensor(out=nfrac[:].rearrange(fl), in0=frac[:].rearrange(fl), scalar=0.5,
+                                       in1=frac[:].rearrange(fl), op0=ALU.is_gt, op1=ALU.subtract)
+        tab = pool.tile([P, 2, 2, 2, 2, ROPE], F32, name="tab")
+        for e in range(2):
+            for h2 in range(2):
+                nc.scalar.activation(out=tab[:, :, 0, :, h2, HALF * e:HALF * (e + 1)],
+                                     in_=nfrac[:, 1].rearrange("p (k i) j -> p k i j", k=2), func=ACT.Sin, scale=-TWO_PI)
+                nc.scalar.activation(out=tab[:, :, 1, :, h2, HALF * e:HALF * (e + 1)],
+                                     in_=nfrac[:, 0].rearrange("p (k i) j -> p k i j", k=2), func=ACT.Sin,
+                                     scale=(-TWO_PI if e == 0 else TWO_PI))
+
+        xt_banks = {}
+        x_grp = {}
+        w_grp = {}
+        acc = {}
+        rope = {}
+        o_tiles = {}
+        o8_tiles = {}
+        stats = {}
+        q_sb = {}
+
+        def copy_on(eng, out, in_):
+            if eng == "V":
+                nc.vector.tensor_copy(out=out, in_=in_)
+            elif eng == "S":
+                nc.scalar.copy(out=out, in_=in_)
+            else:
+                nc.gpsimd.tensor_scalar(out=out, in0=in_, scalar1=1.0, scalar2=0.0, op0=ALU.mult, op1=ALU.add)
+
+        def xtb(b, i, gp):
+            words = x_raw[(b, i)][:].bitcast(F32)
+            bank = psum.tile([P, 2, 2, P], F32, name="xt%d" % gp)
+            for gg in range(2):
+                g = 2 * gp + gg
+                for u in range(2):
+                    nc.tensor.transpose(out=bank[:, gg, u, :], in_=words[:, 256 * g + u:256 * (g + 1):2],
+                                        identity=ident[:])
+            xt_banks[(b, i, gp)] = bank
+
+        def xc(b, i, gp, eng):
+            if (b, i // 2) not in x_grp:
+                x_grp[(b, i // 2)] = pool.tile([P, 2, NG, P, 4], BF16, name="x_grp%d" % (i // 2), align_bytes=64)
+            dst = x_grp[(b, i // 2)][:, i % 2, 2 * gp:2 * gp + 2, :, :].bitcast(F32)
+            copy_on(eng, dst, xt_banks[(b, i, gp)][:].rearrange("p g u r -> p g r u"))
+
+        def xq(b, k):
+            nc.vector.quantize_mx(out=x_codes[:, b, 2 * k:2 * k + 2, :].rearrange("p i w -> p (i w)").bitcast(FP8X4),
+                                  scales=x_scales[:, b, 2 * k:2 * k + 2, :].rearrange("p i w -> p (i w)"),
+                                  in_=x_grp[(b, k)][:].rearrange("p i g r t -> p (i g r t)"))
+
+        def wi(c, g, part, eng):
+            width = W_CHUNKS[c][1]
+            if (c, g // 2) not in w_grp:
+                w_grp[(c, g // 2)] = pool.tile([P, 2, width, 4], BF16, name="w_grp%d_%d" % (width, g // 2), align_bytes=64)
+            dst = w_grp[(c, g // 2)][:, g % 2].rearrange("p (h d) t -> p h d t", d=D)
+            src = w_raw[(c, g)][:].rearrange("p t (h d) -> p h d t", d=D)
+            if part == 0:
+                copy_on(eng, dst[:, :, 0:NOPE, :], src[:, :, 0:NOPE, :])
+            else:
+                e = part - 1
+                copy_on(eng, dst[:, :, NOPE + HALF * e:NOPE + HALF * (e + 1), :], src[:, :, NOPE + e:D:2, :])
+
+        def wq(c, gq):
+            codes, scales = (ws_codes[:, c], ws_scales[:, c]) if c < 2 else (wb_codes[:, c - 2], wb_scales[:, c - 2])
+            nc.vector.quantize_mx(out=codes[:, 2 * gq:2 * gq + 2, :].rearrange("p g w -> p (g w)").bitcast(FP8X4),
+                                  scales=scales[:, 2 * gq:2 * gq + 2, :].rearrange("p g w -> p (g w)"),
+                                  in_=w_grp[(c, gq)][:].rearrange("p g w t -> p (g w t)"))
+
+        def pair_of(m):
+            return m // 4, (m // 2) % 2, m % 2
+
+        def mm(n):
+            nt, b, hp = pair_of(n // 2)
+            a = psum.tile([P, 2, 2 * D], F32, name="acc%d" % (n % NACC))
+            for i2 in range(2):
+                i = 2 * (n % 2) + i2
+                for g in range(NG):
+                    if nt == 0:
+                        rhs, rhs_scale = ws_codes[:, hp, g, :], ws_scales[:, hp, g, :]
+                    else:
+                        rhs = wb_codes[:, nt - 1, g, 256 * hp:256 * (hp + 1)]
+                        rhs_scale = wb_scales[:, nt - 1, g, 256 * hp:256 * (hp + 1)]
+                    nc.tensor.matmul_mx(out=a[:, i2, :], lhsT=x_codes[:, b, i, P * g:P * (g + 1)].bitcast(FP8X4),
+                                        lhsT_scale=x_scales[:, b, i, P * g:P * (g + 1)], rhs=rhs.bitcast(FP8X4),
+                                        rhs_scale=rhs_scale, start=(g == 0), stop=(g == NG - 1))
+            acc[n] = a
+
+        def o32_of(nt, b):
+            if (nt, b) not in o_tiles:
+                o_tiles[(nt, b)] = pool.tile([P, 4, NI, D], F32, name="o32_%d" % ((2 * nt + b) % 3))
+            return o_tiles[(nt, b)]
+
+        def o8_of(nt, b):
+            if (nt, b) not in o8_tiles:
+                o8_tiles[(nt, b)] = pool.tile([P, 4, NI, D], FP8, name="o8_%d" % ((2 * nt + b) % 3))
+            return o8_tiles[(nt, b)]
+
+        def abs_(n):
+            m, k = n // 2, n % 2
+            nt, b, hp = pair_of(m)
+            nc.scalar.copy(out=o32_of(nt, b)[:, 2 * hp:2 * hp + 2, 2 * k:2 * k + 2, 0:NOPE],
+                           in_=acc[n][:].rearrange("p i (h d) -> p h i d", h=2)[:, :, :, 0:NOPE])
+
+        def abv(n):
+            m, k = n // 2, n % 2
+            if m not in rope:
+                rope[m] = pool.tile([P, 2, 2, 4, ROPE], F32, name="rope%d" % (m % 3))
+            q = acc[n][:].rearrange("p i (h d) -> p (i h) d", h=2)[:, :, NOPE:D]
+            nc.vector.tensor_tensor(out=rope[m][:, :, k], in0=tab[:, k].rearrange("p s i h c -> p s (i h) c"),
+                                    in1=q.unsqueeze(1).to_broadcast([P, 2, 4, ROPE]), op=ALU.mult)
+
+        def abq(n):
+            q = acc[n][:].rearrange("p i (h d) -> p (i h) d", h=2)[:, :, NOPE:D]
+            q_sb[n] = pool.tile([P, 4, ROPE], F32, name="q_sb%d" % ((n // 4) % 2))
+            nc.scalar.copy(out=q_sb[n][:], in_=q)
+
+        def abg(n):
+            m, k = n // 2, n % 2
+            if m not in rope:
+                rope[m] = pool.tile([P, 2, 2, 4, ROPE], F32, name="rope%d" % (m % 3))
+            nc.gpsimd.tensor_tensor(out=rope[m][:, :, k], in0=tab[:, k].rearrange("p s i h c -> p s (i h) c"),
+                                    in1=q_sb[n][:].unsqueeze(1).to_broadcast([P, 2, 4, ROPE]), op=ALU.mult)
+
+        def ab(n):
+            if n in GROPE:
+                abq(n)
+                abg(n)
+            else:
+                abv(n)
+            abs_(n)
+
+        def cc(m, eng):
+            nt, b, hp = pair_of(m)
+            o32 = o32_of(nt, b)
+            e = nc.gpsimd if eng == "G" else nc.vector
+            for f in range(2):
+                e.tensor_tensor(out=o32[:, 2 * hp:2 * hp + 2, :, NOPE + HALF * f:NOPE + HALF * (f + 1)],
+                                in0=rope[m][:, 0, :, :, HALF * f:HALF * (f + 1)].rearrange("p k (i h) j -> p h (k i) j", h=2),
+                                in1=rope[m][:, 1, :, :, HALF * (1 - f):HALF * (2 - f)].rearrange("p k (i h) j -> p h (k i) j", h=2),
+                                op=ALU.add)
+
+        def mx(u, h0, nh):
+            nt, b = u // 2, u % 2
+            o32 = o32_of(nt, b)
+            if u not in stats:
+                stats[u] = (pool.tile([P, 16], F32, name="amax%d" % (u % 3)), pool.tile([P, 16], F32, name="rcp%d" % (u % 3)),
+                            pool.tile([P, 16], F32, name="fac%d" % (u % 3)))
+            cols = slice(4 * h0, 4 * (h0 + nh))
+            nc.vector.tensor_reduce(out=stats[u][0][:, cols], in_=o32[:, h0:h0 + nh].rearrange("p h i d -> p (h i) d"),
+                                    axis=AX.X, op=ALU.max, apply_absolute_value=True)
+            nc.vector.reciprocal(out=stats[u][1][:, cols], in_=stats[u][0][:, cols])
+
+        def fs(u, h0, nh):
+            cols = slice(4 * h0, 4 * (h0 + nh))
+            nc.scalar.activation(out=stats[u][2][:, cols], in_=stats[u][1][:, cols], func=ACT.Copy, scale=448.0)
+
+        def fv(u, h0, nh):
+            cols = slice(4 * h0, 4 * (h0 + nh))
+            nc.vector.tensor_scalar(out=stats[u][2][:, cols], in0=stats[u][1][:, cols], scalar1=448.0, scalar2=None,
+                                    op0=ALU.mult)
+
+        def ks(u, r0, r1):
+            nt, b = u // 2, u % 2
+            o32, o8 = o32_of(nt, b), o8_of(nt, b)
+            for r in range(r0, r1):
+                nc.scalar.activation(out=o8[:, r // 4, r % 4, :], in_=o32[:, r // 4, r % 4, :], func=ACT.Identity,
+                                     scale=stats[u][2][:, r:r + 1], bias=zero[:, 0:1], saturate=False)
+
+        def kv(u, r0, r1):
+            nt, b = u // 2, u % 2
+            o32, o8 = o32_of(nt, b), o8_of(nt, b)
+            for r in range(r0, r1):
+                nc.vector.tensor_scalar(out=o8[:, r // 4, r % 4, :], in0=o32[:, r // 4, r % 4, :],
+                                        scalar1=stats[u][2][:, r:r + 1], scalar2=None, op0=ALU.mult, saturate=False)
+
+        def st0(u, h0, nh):
+            nt, b = u // 2, u % 2
+            nc.sync.dma_start(out=out_0[b, 4 * nt + h0:4 * nt + h0 + nh].rearrange("h (p i) d -> p h (i d)", i=NI),
+                              in_=o32_of(nt, b)[:, h0:h0 + nh].rearrange("p h i d -> p h (i d)"))
+
+        def st1(u, h0, nh):
+            nt, b = u // 2, u % 2
+            nc.sync.dma_start(out=out_1[b, 4 * nt + h0:4 * nt + h0 + nh].rearrange("h (p i) d -> p h (i d)", i=NI),
+                              in_=o8_of(nt, b)[:, h0:h0 + nh].bitcast(U8).rearrange("p h i d -> p h (i d)"))
+
+        with tc.manual_schedule():
+            wi(0, 0, 2, "G")
+            xtb(0, 0, 0)
+            wi(0, 1, 2, "V")
+            wi(0, 2, 2, "V")
+            xc(0, 0, 0, "S")
+            wi(0, 2, 1, "V")
+            xtb(0, 0, 1)
+            xc(0, 0, 1, "S")
+            xtb(0, 1, 0)
+            xc(0, 1, 0, "V")
+            xtb(0, 1, 1)
+            xc(0, 1, 1, "V")
+            wi(0, 2, 0, "S")
+            xtb(0, 2, 1)
+            load_x(1, 0)
+            wi(0, 1, 0, "S")
+            xtb(0, 2, 0)
+            wi(0, 1, 1, "G")
+            wi(0, 0, 1, "S")
+            load_x(1, 1)
+            load_w(2, 0)
+            wi(0, 0, 0, "S")
+            wi(0, 3, 2, "S")
+            wi(0, 3, 0, "S")
+            xc(0, 2, 1, "S")
+            wi(0, 3, 1, "V")
+            xq(0, 0)
+            wq(0, 0)
+            xc(0, 2, 0, "V")
+            wq(0, 1)
+            wi(1, 0, 0, "S")
+            xtb(0, 3, 1)
+            xtb(0, 3, 0)
+            wi(1, 1, 1, "S")
+            wi(1, 0, 2, "V")
+            wi(1, 2, 0, "S")
+            wi(1, 3, 1, "S")
+            load_x(1, 2)
+            wi(1, 2, 2, "V")
+            mm(0)
+            xc(0, 3, 0, "V")
+            xtb(1, 0, 0)
+            wi(1, 0, 1, "S")
+            xc(0, 3, 1, "V")
+            wi(1, 1, 2, "G")
+            wi(1, 1, 0, "S")
+            xtb(1, 0, 1)
+            xc(1, 0, 0, "S")
+            xc(1, 0, 1, "S")
+            abv(0)
+            load_w(2, 1)
+            wi(1, 3, 2, "S")
+            load_w(2, 2)
+            wi(1, 2, 1, "G")
+            xtb(1, 1, 0)
+            load_x(1, 3)
+            xc(1, 1, 0, "S")
+            xtb(1, 1, 1)
+            load_w(2, 3)
+            wi(1, 3, 0, "V")
+            xc(1, 1, 1, "S")
+            load_w(3, 0)
+            wq(1, 0)
+            wi(2, 0, 0, "S")
+            xq(0, 1)
+            wi(2, 0, 1, "V")
+            wi(2, 0, 2, "V")
+            xtb(1, 2, 0)
+            xtb(1, 2, 1)
+            wq(1, 1)
+            wi(2, 1, 2, "S")
+            xc(1, 2, 1, "S")
+            xq(1, 0)
+            mm(2)
+            xc(1, 2, 0, "S")
+            mm(1)
+            wi(2, 1, 1, "V")
+            wi(2, 2, 0, "S")
+            wi(2, 1, 0, "V")
+            xtb(1, 3, 1)
+            load_w(3, 1)
+            wi(2, 2, 1, "S")
+            xtb(1, 3, 0)
+            wq(2, 0)
+            abv(1)
+            wi(2, 2, 2, "G")
+            load_w(4, 1)
+            load_w(3, 2)
+            xc(1, 3, 0, "S")
+            xc(1, 3, 1, "V")
+            wi(2, 3, 1, "S")
+            xq(1, 1)
+            mm(4)
+            mm(5)
+            abs_(1)
+            abs_(0)
+            load_w(3, 3)
+            cc(0, "G")
+            abv(2)
+            wi(2, 3, 0, "S")
+            wi(2, 3, 2, "S")
+            wi(3, 0, 1, "S")
+            mm(3)
+            abv(4)
+            abs_(2)
+            wq(2, 1)
+            wi(3, 0, 2, "S")
+            wi(3, 1, 2, "G")
+            mm(7)
+            abv(3)
+            wi(3, 1, 0, "S")
+            mm(6)
+            abs_(3)
+            cc(1, "G")
+            wi(3, 1, 1, "S")
+            abv(5)
+            wi(3, 2, 0, "S")
+            wi(3, 0, 0, "S")
+            wi(3, 2, 1, "S")
+            mm(9)
+            abs_(4)
+            abs_(5)
+            abv(6)
+            mm(8)
+            wi(3, 3, 0, "S")
+            wi(3, 3, 2, "S")
+            abv(7)
+            abs_(7)
+            mm(11)
+            mm(10)
+            wi(3, 3, 1, "S")
+            wi(3, 2, 2, "S")
+            abv(9)
+            load_w(4, 0)
+            abv(8)
+            load_w(4, 2)
+            cc(2, "G")
+            abs_(6)
+            mm(12)
+            wq(3, 0)
+            abs_(9)
+            cc(4, "G")
+            abv(11)
+            wi(4, 1, 0, "S")
+            mx(0, 0, 4)
+            abv(10)
+            st0(0, 0, 4)
+            cc(3, "G")
+            wi(4, 0, 0, "S")
+            wq(3, 1)
+            cc(5, "G")
+            wi(4, 0, 1, "S")
+            abs_(8)
+            wi(4, 1, 1, "G")
+            wi(4, 0, 2, "S")
+            mm(14)
+            mm(15)
+            wi(4, 1, 2, "S")
+            abs_(11)
+            load_w(4, 3)
+            mx(1, 0, 4)
+            abv(15)
+            abv(14)
+            wi(4, 2, 2, "S")
+            fs(0, 0, 4)
+            st0(1, 0, 4)
+            wi(4, 2, 1, "G")
+            mm(17)
+            fs(1, 0, 4)
+            wi(4, 3, 1, "S")
+            abs_(10)
+            wi(4, 2, 0, "S")
+            st0(2, 0, 4)
+            mm(13)
+            ks(0, 8, 16)
+            wi(4, 3, 0, "S")
+            abv(13)
+            mm(16)
+            wi(4, 3, 2, "G")
+            ks(0, 0, 8)
+            abv(12)
+            wq(4, 0)
+            wq(4, 1)
+            abs_(12)
+            abs_(14)
+            mm(18)
+            abv(16)
+            ks(1, 8, 16)
+            cc(7, "G")
+            abv(17)
+            abs_(15)
+            abs_(13)
+            ks(1, 0, 8)
+            mm(21)
+            mx(2, 0, 4)
+            abq(21)
+            mm(20)
+            fs(2, 0, 4)
+            cc(6, "G")
+            abv(18)
+            abv(20)
+            st1(0, 0, 4)
+            mx(3, 0, 4)
+            abs_(16)
+            abs_(17)
+            mm(22)
+            ks(2, 8, 16)
+            ks(2, 0, 8)
+            st0(3, 0, 4)
+            abg(21)
+            abs_(18)
+            mm(23)
+            mm(19)
+            abs_(21)
+            fs(3, 0, 4)
+            cc(8, "G")
+            abv(19)
+            ks(3, 8, 16)
+            abs_(19)
+            mm(27)
+            abv(23)
+            cc(10, "G")
+            abs_(20)
+            ks(3, 0, 8)
+            abv(22)
+            cc(9, "G")
+            abv(27)
+            mm(24)
+            st1(1, 0, 4)
+            mm(26)
+            st1(2, 0, 4)
+            mm(25)
+            abs_(22)
+            abq(25)
+            cc(11, "G")
+            mx(4, 0, 4)
+            abg(25)
+            abs_(27)
+            abv(24)
+            abs_(25)
+            fs(4, 0, 4)
+            abs_(23)
+            abv(26)
+            mm(29)
+            mx(5, 0, 4)
+            ks(4, 0, 8)
+            abs_(24)
+            abq(29)
+            mm(28)
+            mm(30)
+            cc(12, "G")
+            abs_(26)
+            st1(3, 0, 4)
+            st0(4, 0, 4)
+            ks(4, 8, 16)
+            abv(28)
+            st0(5, 0, 4)
+            mm(31)
+            cc(13, "G")
+            abv(30)
+            fs(5, 0, 4)
+            st1(4, 0, 4)
+            abs_(29)
+            abg(29)
+            ks(5, 0, 8)
+            abs_(30)
+            ks(5, 8, 16)
+            mx(6, 0, 4)
+            abs_(28)
+            fs(6, 0, 4)
+            st0(6, 0, 4)
+            ks(6, 0, 8)
+            cc(14, "G")
+            st1(5, 0, 4)
+            abv(31)
+            mx(7, 0, 2)
+            cc(15, "G")
+            abs_(31)
+            mx(7, 2, 2)
+            ks(6, 8, 16)
+            st0(7, 0, 2)
+            fv(7, 2, 2)
+            fs(7, 0, 2)
+            ks(7, 0, 8)
+            st0(7, 2, 2)
+            st1(6, 0, 4)
+            ks(7, 13, 16)
+            kv(7, 8, 13)
+            st1(7, 0, 2)
+            st1(7, 2, 2)

@@ -32,6 +32,7 @@ def tile_mla_pb_kernel(tc, x, Wq, out_0, out_1):
     with ExitStack() as ctx:
         pool = ctx.enter_context(tc.tile_pool(name="sb", bufs=1))
         psum = ctx.enter_context(tc.psum_pool(name="ps", bufs=1))
+        ctx.enter_context(tc.manual_schedule())
 
         x_codes = pool.tile([P, NB, NI, NG * P], U32, name="x_codes", align_bytes=64)
         x_scales = pool.tile([P, NB, NI, NG * P], U8, name="x_scales", align_bytes=64)
@@ -275,294 +276,293 @@ def tile_mla_pb_kernel(tc, x, Wq, out_0, out_1):
             nc.sync.dma_start(out=out_1[b, 4 * nt + h0:4 * nt + h0 + nh].rearrange("h (p i) d -> p h (i d)", i=NI),
                               in_=o8_of(nt, b)[:, h0:h0 + nh].bitcast(U8).rearrange("p h i d -> p h (i d)"))
 
-        with tc.manual_schedule():
-            wi(0, 0, 2, "G")
-            xtb(0, 0, 0)
-            wi(0, 1, 2, "V")
-            wi(0, 2, 2, "V")
-            xc(0, 0, 0, "S")
-            wi(0, 2, 1, "V")
-            xtb(0, 0, 1)
-            xc(0, 0, 1, "S")
-            xtb(0, 1, 0)
-            xc(0, 1, 0, "V")
-            xtb(0, 1, 1)
-            xc(0, 1, 1, "V")
-            wi(0, 2, 0, "S")
-            xtb(0, 2, 1)
-            load_x(1, 0)
-            wi(0, 1, 0, "S")
-            xtb(0, 2, 0)
-            wi(0, 1, 1, "G")
-            wi(0, 0, 1, "S")
-            load_x(1, 1)
-            load_w(2, 0)
-            wi(0, 0, 0, "S")
-            wi(0, 3, 2, "S")
-            wi(0, 3, 0, "S")
-            xc(0, 2, 1, "S")
-            wi(0, 3, 1, "V")
-            xq(0, 0)
-            wq(0, 0)
-            xc(0, 2, 0, "V")
-            wq(0, 1)
-            wi(1, 0, 0, "S")
-            xtb(0, 3, 1)
-            xtb(0, 3, 0)
-            wi(1, 1, 1, "S")
-            wi(1, 0, 2, "V")
-            wi(1, 2, 0, "S")
-            wi(1, 3, 1, "S")
-            load_x(1, 2)
-            wi(1, 2, 2, "V")
-            mm(0)
-            xc(0, 3, 0, "V")
-            xtb(1, 0, 0)
-            wi(1, 0, 1, "S")
-            xc(0, 3, 1, "V")
-            wi(1, 1, 2, "G")
-            wi(1, 1, 0, "S")
-            xtb(1, 0, 1)
-            xc(1, 0, 0, "S")
-            xc(1, 0, 1, "S")
-            abv(0)
-            load_w(2, 1)
-            wi(1, 3, 2, "S")
-            load_w(2, 2)
-            wi(1, 2, 1, "G")
-            xtb(1, 1, 0)
-            load_x(1, 3)
-            xc(1, 1, 0, "S")
-            xtb(1, 1, 1)
-            load_w(2, 3)
-            wi(1, 3, 0, "V")
-            xc(1, 1, 1, "S")
-            load_w(3, 0)
-            wq(1, 0)
-            wi(2, 0, 0, "S")
-            xq(0, 1)
-            wi(2, 0, 1, "V")
-            wi(2, 0, 2, "V")
-            xtb(1, 2, 0)
-            xtb(1, 2, 1)
-            wq(1, 1)
-            wi(2, 1, 2, "S")
-            xc(1, 2, 1, "S")
-            xq(1, 0)
-            mm(2)
-            xc(1, 2, 0, "S")
-            mm(1)
-            wi(2, 1, 1, "V")
-            wi(2, 2, 0, "S")
-            wi(2, 1, 0, "V")
-            xtb(1, 3, 1)
-            load_w(3, 1)
-            wi(2, 2, 1, "S")
-            xtb(1, 3, 0)
-            wq(2, 0)
-            abv(1)
-            wi(2, 2, 2, "G")
-            load_w(4, 1)
-            load_w(3, 2)
-            xc(1, 3, 0, "S")
-            xc(1, 3, 1, "V")
-            wi(2, 3, 1, "S")
-            xq(1, 1)
-            mm(4)
-            mm(5)
-            abs_(1)
-            abs_(0)
-            load_w(3, 3)
-            cc(0, "G")
-            abv(2)
-            wi(2, 3, 0, "S")
-            wi(2, 3, 2, "S")
-            wi(3, 0, 1, "S")
-            mm(3)
-            abv(4)
-            abs_(2)
-            wq(2, 1)
-            wi(3, 0, 2, "S")
-            wi(3, 1, 2, "G")
-            mm(7)
-            abv(3)
-            wi(3, 1, 0, "S")
-            mm(6)
-            abs_(3)
-            cc(1, "G")
-            wi(3, 1, 1, "S")
-            abv(5)
-            wi(3, 2, 0, "S")
-            wi(3, 0, 0, "S")
-            wi(3, 2, 1, "S")
-            mm(9)
-            abs_(4)
-            abs_(5)
-            abv(6)
-            mm(8)
-            wi(3, 3, 0, "S")
-            wi(3, 3, 2, "S")
-            abv(7)
-            abs_(7)
-            mm(11)
-            mm(10)
-            wi(3, 3, 1, "S")
-            wi(3, 2, 2, "S")
-            abv(9)
-            load_w(4, 0)
-            abv(8)
-            load_w(4, 2)
-            cc(2, "G")
-            abs_(6)
-            mm(12)
-            wq(3, 0)
-            abs_(9)
-            cc(4, "G")
-            abv(11)
-            wi(4, 1, 0, "S")
-            mx(0, 0, 4)
-            abv(10)
-            st0(0, 0, 4)
-            cc(3, "G")
-            wi(4, 0, 0, "S")
-            wq(3, 1)
-            cc(5, "G")
-            wi(4, 0, 1, "S")
-            abs_(8)
-            wi(4, 1, 1, "G")
-            wi(4, 0, 2, "S")
-            mm(14)
-            mm(15)
-            wi(4, 1, 2, "S")
-            abs_(11)
-            load_w(4, 3)
-            mx(1, 0, 4)
-            abv(15)
-            abv(14)
-            wi(4, 2, 2, "S")
-            fs(0, 0, 4)
-            st0(1, 0, 4)
-            wi(4, 2, 1, "G")
-            mm(17)
-            fs(1, 0, 4)
-            wi(4, 3, 1, "S")
-            abs_(10)
-            wi(4, 2, 0, "S")
-            st0(2, 0, 4)
-            mm(13)
-            ks(0, 8, 16)
-            wi(4, 3, 0, "S")
-            abv(13)
-            mm(16)
-            wi(4, 3, 2, "G")
-            ks(0, 0, 8)
-            abv(12)
-            wq(4, 0)
-            wq(4, 1)
-            abs_(12)
-            abs_(14)
-            mm(18)
-            abv(16)
-            ks(1, 8, 16)
-            cc(7, "G")
-            abv(17)
-            abs_(15)
-            abs_(13)
-            ks(1, 0, 8)
-            mm(21)
-            mx(2, 0, 4)
-            abq(21)
-            mm(20)
-            fs(2, 0, 4)
-            cc(6, "G")
-            abv(18)
-            abv(20)
-            st1(0, 0, 4)
-            mx(3, 0, 4)
-            abs_(16)
-            abs_(17)
-            mm(22)
-            ks(2, 8, 16)
-            ks(2, 0, 8)
-            st0(3, 0, 4)
-            abg(21)
-            abs_(18)
-            mm(23)
-            mm(19)
-            abs_(21)
-            fs(3, 0, 4)
-            cc(8, "G")
-            abv(19)
-            ks(3, 8, 16)
-            abs_(19)
-            mm(27)
-            abv(23)
-            cc(10, "G")
-            abs_(20)
-            ks(3, 0, 8)
-            abv(22)
-            cc(9, "G")
-            abv(27)
-            mm(24)
-            st1(1, 0, 4)
-            mm(26)
-            st1(2, 0, 4)
-            mm(25)
-            abs_(22)
-            abq(25)
-            cc(11, "G")
-            mx(4, 0, 4)
-            abg(25)
-            abs_(27)
-            abv(24)
-            abs_(25)
-            fs(4, 0, 4)
-            abs_(23)
-            abv(26)
-            mm(29)
-            mx(5, 0, 4)
-            ks(4, 0, 8)
-            abs_(24)
-            abq(29)
-            mm(28)
-            mm(30)
-            cc(12, "G")
-            abs_(26)
-            st1(3, 0, 4)
-            st0(4, 0, 4)
-            ks(4, 8, 16)
-            abv(28)
-            st0(5, 0, 4)
-            mm(31)
-            cc(13, "G")
-            abv(30)
-            fs(5, 0, 4)
-            st1(4, 0, 4)
-            abs_(29)
-            abg(29)
-            ks(5, 0, 8)
-            abs_(30)
-            ks(5, 8, 16)
-            mx(6, 0, 4)
-            abs_(28)
-            fs(6, 0, 4)
-            st0(6, 0, 4)
-            ks(6, 0, 8)
-            cc(14, "G")
-            st1(5, 0, 4)
-            abv(31)
-            mx(7, 0, 2)
-            cc(15, "G")
-            abs_(31)
-            mx(7, 2, 2)
-            ks(6, 8, 16)
-            st0(7, 0, 2)
-            fv(7, 2, 2)
-            fs(7, 0, 2)
-            ks(7, 0, 8)
-            st0(7, 2, 2)
-            st1(6, 0, 4)
-            ks(7, 13, 16)
-            kv(7, 8, 13)
-            st1(7, 0, 2)
-            st1(7, 2, 2)
+        wi(0, 0, 2, "G")
+        xtb(0, 0, 0)
+        wi(0, 1, 2, "V")
+        wi(0, 2, 2, "V")
+        xc(0, 0, 0, "S")
+        wi(0, 2, 1, "V")
+        xtb(0, 0, 1)
+        xc(0, 0, 1, "S")
+        xtb(0, 1, 0)
+        xc(0, 1, 0, "V")
+        xtb(0, 1, 1)
+        xc(0, 1, 1, "V")
+        wi(0, 2, 0, "S")
+        xtb(0, 2, 1)
+        load_x(1, 0)
+        wi(0, 1, 0, "S")
+        xtb(0, 2, 0)
+        wi(0, 1, 1, "G")
+        wi(0, 0, 1, "S")
+        load_x(1, 1)
+        load_w(2, 0)
+        wi(0, 0, 0, "S")
+        wi(0, 3, 2, "S")
+        wi(0, 3, 0, "S")
+        xc(0, 2, 1, "S")
+        wi(0, 3, 1, "V")
+        xq(0, 0)
+        wq(0, 0)
+        xc(0, 2, 0, "V")
+        wq(0, 1)
+        wi(1, 0, 0, "S")
+        xtb(0, 3, 1)
+        xtb(0, 3, 0)
+        wi(1, 1, 1, "S")
+        wi(1, 0, 2, "V")
+        wi(1, 2, 0, "S")
+        wi(1, 3, 1, "S")
+        load_x(1, 2)
+        wi(1, 2, 2, "V")
+        mm(0)
+        xc(0, 3, 0, "V")
+        xtb(1, 0, 0)
+        wi(1, 0, 1, "S")
+        xc(0, 3, 1, "V")
+        wi(1, 1, 2, "G")
+        wi(1, 1, 0, "S")
+        xtb(1, 0, 1)
+        xc(1, 0, 0, "S")
+        xc(1, 0, 1, "S")
+        abv(0)
+        load_w(2, 1)
+        wi(1, 3, 2, "S")
+        load_w(2, 2)
+        wi(1, 2, 1, "G")
+        xtb(1, 1, 0)
+        load_x(1, 3)
+        xc(1, 1, 0, "S")
+        xtb(1, 1, 1)
+        load_w(2, 3)
+        wi(1, 3, 0, "V")
+        xc(1, 1, 1, "S")
+        load_w(3, 0)
+        wq(1, 0)
+        wi(2, 0, 0, "S")
+        xq(0, 1)
+        wi(2, 0, 1, "V")
+        wi(2, 0, 2, "V")
+        xtb(1, 2, 0)
+        xtb(1, 2, 1)
+        wq(1, 1)
+        wi(2, 1, 2, "S")
+        xc(1, 2, 1, "S")
+        xq(1, 0)
+        mm(2)
+        xc(1, 2, 0, "S")
+        mm(1)
+        wi(2, 1, 1, "V")
+        wi(2, 2, 0, "S")
+        wi(2, 1, 0, "V")
+        xtb(1, 3, 1)
+        load_w(3, 1)
+        wi(2, 2, 1, "S")
+        xtb(1, 3, 0)
+        wq(2, 0)
+        abv(1)
+        wi(2, 2, 2, "G")
+        load_w(4, 1)
+        load_w(3, 2)
+        xc(1, 3, 0, "S")
+        xc(1, 3, 1, "V")
+        wi(2, 3, 1, "S")
+        xq(1, 1)
+        mm(4)
+        mm(5)
+        abs_(1)
+        abs_(0)
+        load_w(3, 3)
+        cc(0, "G")
+        abv(2)
+        wi(2, 3, 0, "S")
+        wi(2, 3, 2, "S")
+        wi(3, 0, 1, "S")
+        mm(3)
+        abv(4)
+        abs_(2)
+        wq(2, 1)
+        wi(3, 0, 2, "S")
+        wi(3, 1, 2, "G")
+        mm(7)
+        abv(3)
+        wi(3, 1, 0, "S")
+        mm(6)
+        abs_(3)
+        cc(1, "G")
+        wi(3, 1, 1, "S")
+        abv(5)
+        wi(3, 2, 0, "S")
+        wi(3, 0, 0, "S")
+        wi(3, 2, 1, "S")
+        mm(9)
+        abs_(4)
+        abs_(5)
+        abv(6)
+        mm(8)
+        wi(3, 3, 0, "S")
+        wi(3, 3, 2, "S")
+        abv(7)
+        abs_(7)
+        mm(11)
+        mm(10)
+        wi(3, 3, 1, "S")
+        wi(3, 2, 2, "S")
+        abv(9)
+        load_w(4, 0)
+        abv(8)
+        load_w(4, 2)
+        cc(2, "G")
+        abs_(6)
+        mm(12)
+        wq(3, 0)
+        abs_(9)
+        cc(4, "G")
+        abv(11)
+        wi(4, 1, 0, "S")
+        mx(0, 0, 4)
+        abv(10)
+        st0(0, 0, 4)
+        cc(3, "G")
+        wi(4, 0, 0, "S")
+        wq(3, 1)
+        cc(5, "G")
+        wi(4, 0, 1, "S")
+        abs_(8)
+        wi(4, 1, 1, "G")
+        wi(4, 0, 2, "S")
+        mm(14)
+        mm(15)
+        wi(4, 1, 2, "S")
+        abs_(11)
+        load_w(4, 3)
+        mx(1, 0, 4)
+        abv(15)
+        abv(14)
+        wi(4, 2, 2, "S")
+        fs(0, 0, 4)
+        st0(1, 0, 4)
+        wi(4, 2, 1, "G")
+        mm(17)
+        fs(1, 0, 4)
+        wi(4, 3, 1, "S")
+        abs_(10)
+        wi(4, 2, 0, "S")
+        st0(2, 0, 4)
+        mm(13)
+        ks(0, 8, 16)
+        wi(4, 3, 0, "S")
+        abv(13)
+        mm(16)
+        wi(4, 3, 2, "G")
+        ks(0, 0, 8)
+        abv(12)
+        wq(4, 0)
+        wq(4, 1)
+        abs_(12)
+        abs_(14)
+        mm(18)
+        abv(16)
+        ks(1, 8, 16)
+        cc(7, "G")
+        abv(17)
+        abs_(15)
+        abs_(13)
+        ks(1, 0, 8)
+        mm(21)
+        mx(2, 0, 4)
+        abq(21)
+        mm(20)
+        fs(2, 0, 4)
+        cc(6, "G")
+        abv(18)
+        abv(20)
+        st1(0, 0, 4)
+        mx(3, 0, 4)
+        abs_(16)
+        abs_(17)
+        mm(22)
+        ks(2, 8, 16)
+        ks(2, 0, 8)
+        st0(3, 0, 4)
+        abg(21)
+        abs_(18)
+        mm(23)
+        mm(19)
+        abs_(21)
+        fs(3, 0, 4)
+        cc(8, "G")
+        abv(19)
+        ks(3, 8, 16)
+        abs_(19)
+        mm(27)
+        abv(23)
+        cc(10, "G")
+        abs_(20)
+        ks(3, 0, 8)
+        abv(22)
+        cc(9, "G")
+        abv(27)
+        mm(24)
+        st1(1, 0, 4)
+        mm(26)
+        st1(2, 0, 4)
+        mm(25)
+        abs_(22)
+        abq(25)
+        cc(11, "G")
+        mx(4, 0, 4)
+        abg(25)
+        abs_(27)
+        abv(24)
+        abs_(25)
+        fs(4, 0, 4)
+        abs_(23)
+        abv(26)
+        mm(29)
+        mx(5, 0, 4)
+        ks(4, 0, 8)
+        abs_(24)
+        abq(29)
+        mm(28)
+        mm(30)
+        cc(12, "G")
+        abs_(26)
+        st1(3, 0, 4)
+        st0(4, 0, 4)
+        ks(4, 8, 16)
+        abv(28)
+        st0(5, 0, 4)
+        mm(31)
+        cc(13, "G")
+        abv(30)
+        fs(5, 0, 4)
+        st1(4, 0, 4)
+        abs_(29)
+        abg(29)
+        ks(5, 0, 8)
+        abs_(30)
+        ks(5, 8, 16)
+        mx(6, 0, 4)
+        abs_(28)
+        fs(6, 0, 4)
+        st0(6, 0, 4)
+        ks(6, 0, 8)
+        cc(14, "G")
+        st1(5, 0, 4)
+        abv(31)
+        mx(7, 0, 2)
+        cc(15, "G")
+        abs_(31)
+        mx(7, 2, 2)
+        ks(6, 8, 16)
+        st0(7, 0, 2)
+        fv(7, 2, 2)
+        fs(7, 0, 2)
+        ks(7, 0, 8)
+        st0(7, 2, 2)
+        st1(6, 0, 4)
+        ks(7, 13, 16)
+        kv(7, 8, 13)
+        st1(7, 0, 2)
+        st1(7, 2, 2)

@@ -94,13 +94,15 @@ def tile_mla_pb_kernel(tc, x, Wq, out_0, out_1):
         nc.vector.scalar_tensor_tensor(out=nfrac[:].rearrange(fl), in0=frac[:].rearrange(fl), scalar=0.5,
                                        in1=frac[:].rearrange(fl), op0=ALU.is_gt, op1=ALU.subtract)
         tab = pool.tile([P, 2, 2, 2, 2, ROPE], F32, name="tab")
-        for e in range(2):
-            for h2 in range(2):
-                nc.scalar.activation(out=tab[:, :, 0, :, h2, HALF * e:HALF * (e + 1)],
-                                     in_=nfrac[:, 1].rearrange("p (k i) j -> p k i j", k=2), func=ACT.Sin, scale=-TWO_PI)
-                nc.scalar.activation(out=tab[:, :, 1, :, h2, HALF * e:HALF * (e + 1)],
-                                     in_=nfrac[:, 0].rearrange("p (k i) j -> p k i j", k=2), func=ACT.Sin,
-                                     scale=(-TWO_PI if e == 0 else TWO_PI))
+
+        def sin_tables():
+            for e in range(2):
+                for h2 in range(2):
+                    nc.scalar.activation(out=tab[:, :, 0, :, h2, HALF * e:HALF * (e + 1)],
+                                         in_=nfrac[:, 1].rearrange("p (k i) j -> p k i j", k=2), func=ACT.Sin, scale=-TWO_PI)
+                    nc.scalar.activation(out=tab[:, :, 1, :, h2, HALF * e:HALF * (e + 1)],
+                                         in_=nfrac[:, 0].rearrange("p (k i) j -> p k i j", k=2), func=ACT.Sin,
+                                         scale=(-TWO_PI if e == 0 else TWO_PI))
 
         xt_banks = {}
         x_grp = {}
@@ -301,6 +303,7 @@ def tile_mla_pb_kernel(tc, x, Wq, out_0, out_1):
         wi(0, 3, 2, "S")
         wi(0, 3, 0, "S")
         xc(0, 2, 1, "S")
+        sin_tables()
         wi(0, 3, 1, "V")
         xq(0, 0)
         wq(0, 0)

@@ -280,16 +280,16 @@ def tile_mla_pb_kernel(tc, x, Wq, out_0, out_1):
 
         wi(0, 0, 2, "G")
         xtb(0, 0, 0)
-        wi(0, 1, 2, "V")
-        wi(0, 2, 2, "V")
         xc(0, 0, 0, "S")
-        wi(0, 2, 1, "V")
         xtb(0, 0, 1)
         xc(0, 0, 1, "S")
         xtb(0, 1, 0)
         xc(0, 1, 0, "V")
         xtb(0, 1, 1)
         xc(0, 1, 1, "V")
+        wi(0, 1, 2, "V")
+        wi(0, 2, 2, "V")
+        wi(0, 2, 1, "V")
         wi(0, 2, 0, "S")
         xtb(0, 2, 1)
         load_x(1, 0)
@@ -476,14 +476,14 @@ def tile_mla_pb_kernel(tc, x, Wq, out_0, out_1):
         mx(2, 0, 4)
         abq(21)
         mm(20)
+        abs_(16)
+        abs_(17)
         fs(2, 0, 4)
         cc(6, "G")
         abv(18)
         abv(20)
         st1(0, 0, 4)
         mx(3, 0, 4)
-        abs_(16)
-        abs_(17)
         mm(22)
         ks(2, 8, 16)
         ks(2, 0, 8)
@@ -493,6 +493,7 @@ def tile_mla_pb_kernel(tc, x, Wq, out_0, out_1):
         mm(23)
         mm(19)
         abs_(21)
+        abs_(20)
         fs(3, 0, 4)
         cc(8, "G")
         abv(19)
@@ -501,7 +502,6 @@ def tile_mla_pb_kernel(tc, x, Wq, out_0, out_1):
         mm(27)
         abv(23)
         cc(10, "G")
-        abs_(20)
         ks(3, 0, 8)
         abv(22)
         cc(9, "G")
@@ -519,8 +519,8 @@ def tile_mla_pb_kernel(tc, x, Wq, out_0, out_1):
         abs_(27)
         abv(24)
         abs_(25)
-        fs(4, 0, 4)
         abs_(23)
+        fs(4, 0, 4)
         abv(26)
         mm(29)
         mx(5, 0, 4)
@@ -539,9 +539,9 @@ def tile_mla_pb_kernel(tc, x, Wq, out_0, out_1):
         mm(31)
         cc(13, "G")
         abv(30)
+        abs_(29)
         fs(5, 0, 4)
         st1(4, 0, 4)
-        abs_(29)
         abg(29)
         ks(5, 0, 8)
         abs_(30)

@@ -124,7 +124,7 @@ def tile_mla_pb_kernel(tc, x, Wq, out_0, out_1):
 
         def xtb(b, i, gp):
             words = x_raw[(b, i)][:].bitcast(F32)
-            bank = psum.tile([P, 2, 2, P], F32, name="xt%d" % gp)
+            bank = psum.tile([P, 2, 2, P], F32, name=("xt%d" % gp) if i % 2 == 0 else ("acc%d" % (4 + gp)))
             for gg in range(2):
                 g = 2 * gp + gg
                 for u in range(2):

@@ -25,6 +25,9 @@ TWO_PI = 6.283185307179586
 RHO = 10000.0 ** (-1.0 / 48.0)
 NACC = 6
 GROPE = (21, 25, 29)
+RC_LATER = (3, 4, 5,)
+MERGE_FROM = 6
+SPLIT_TO = 0
 
 
 def tile_mla_pb_kernel(tc, x, Wq, out_0, out_1):
@@ -228,11 +231,19 @@ def tile_mla_pb_kernel(tc, x, Wq, out_0, out_1):
             nt, b, hp = pair_of(m)
             o32 = o32_of(nt, b)
             e = nc.gpsimd if eng == "G" else nc.vector
-            for f in range(2):
-                e.tensor_tensor(out=o32[:, 2 * hp:2 * hp + 2, :, NOPE + HALF * f:NOPE + HALF * (f + 1)],
-                                in0=rope[m][:, 0, :, :, HALF * f:HALF * (f + 1)].rearrange("p k (i h) j -> p h (k i) j", h=2),
-                                in1=rope[m][:, 1, :, :, HALF * (1 - f):HALF * (2 - f)].rearrange("p k (i h) j -> p h (k i) j", h=2),
+            if m >= MERGE_FROM:
+                e.tensor_tensor(out=o32[:, 2 * hp:2 * hp + 2, :, NOPE:D].rearrange("p h r (f j) -> p r h f j", f=2),
+                                in0=rope[m][:, 0].rearrange("p k (i h) (f j) -> p (k i) h f j", h=2, f=2),
+                                in1=rope[m][:, 1].rearrange("p k (i h) (f j) -> p (k i) h f j", h=2, f=2)[:, :, :, ::-1, :],
                                 op=ALU.add)
+                return
+            for f in range(2):
+                for h in (range(2) if m < SPLIT_TO else (None,)):
+                    hs = slice(0, 2) if h is None else slice(h, h + 1)
+                    e.tensor_tensor(out=o32[:, 2 * hp:2 * hp + 2, :, NOPE + HALF * f:NOPE + HALF * (f + 1)][:, hs],
+                                    in0=rope[m][:, 0, :, :, HALF * f:HALF * (f + 1)].rearrange("p k (i h) j -> p h (k i) j", h=2)[:, hs],
+                                    in1=rope[m][:, 1, :, :, HALF * (1 - f):HALF * (2 - f)].rearrange("p k (i h) j -> p h (k i) j", h=2)[:, hs],
+                                    op=ALU.add)
 
         def mx(u, h0, nh):
             nt, b = u // 2, u % 2
@@ -243,6 +254,11 @@ def tile_mla_pb_kernel(tc, x, Wq, out_0, out_1):
             cols = slice(4 * h0, 4 * (h0 + nh))
             nc.vector.tensor_reduce(out=stats[u][0][:, cols], in_=o32[:, h0:h0 + nh].rearrange("p h i d -> p (h i) d"),
                                     axis=AX.X, op=ALU.max, apply_absolute_value=True)
+            if u not in RC_LATER:
+                nc.vector.reciprocal(out=stats[u][1][:, cols], in_=stats[u][0][:, cols])
+
+        def rc(u, h0, nh):
+            cols = slice(4 * h0, 4 * (h0 + nh))
             nc.vector.reciprocal(out=stats[u][1][:, cols], in_=stats[u][0][:, cols])
 
         def fs(u, h0, nh):
@@ -368,7 +384,7 @@ def tile_mla_pb_kernel(tc, x, Wq, out_0, out_1):
         load_w(4, 1)
         load_w(3, 2)
         xc(1, 3, 0, "S")
-        xc(1, 3, 1, "V")
+        xc(1, 3, 1, "S")
         wi(2, 3, 1, "S")
         xq(1, 1)
         mm(4)
@@ -494,9 +510,10 @@ def tile_mla_pb_kernel(tc, x, Wq, out_0, out_1):
         mm(19)
         abs_(21)
         abs_(20)
-        fs(3, 0, 4)
         cc(8, "G")
         abv(19)
+        rc(3, 0, 4)
+        fs(3, 0, 4)
         ks(3, 8, 16)
         abs_(19)
         mm(27)
@@ -518,6 +535,7 @@ def tile_mla_pb_kernel(tc, x, Wq, out_0, out_1):
         abg(25)
         abs_(27)
         abv(24)
+        rc(4, 0, 4)
         abs_(25)
         abs_(23)
         fs(4, 0, 4)
@@ -535,6 +553,7 @@ def tile_mla_pb_kernel(tc, x, Wq, out_0, out_1):
         st0(4, 0, 4)
         ks(4, 8, 16)
         abv(28)
+        rc(5, 0, 4)
         st0(5, 0, 4)
         mm(31)
         cc(13, "G")

@@ -346,11 +346,11 @@ def tile_mla_pb_kernel(tc, x, Wq, out_0, out_1):
         xc(1, 0, 1, "S")
         abv(0)
         load_w(2, 1)
+        load_x(1, 3)
         wi(1, 3, 2, "S")
         load_w(2, 2)
         wi(1, 2, 1, "G")
         xtb(1, 1, 0)
-        load_x(1, 3)
         xc(1, 1, 0, "S")
         xtb(1, 1, 1)
         load_w(2, 3)
@@ -558,6 +558,7 @@ def tile_mla_pb_kernel(tc, x, Wq, out_0, out_1):
         mm(31)
         cc(13, "G")
         abv(30)
+        abv(31)
         abs_(29)
         fs(5, 0, 4)
         st1(4, 0, 4)
@@ -565,17 +566,18 @@ def tile_mla_pb_kernel(tc, x, Wq, out_0, out_1):
         ks(5, 0, 8)
         abs_(30)
         ks(5, 8, 16)
-        mx(6, 0, 4)
+        mx(6, 0, 2)
+        mx(6, 2, 2)
         abs_(28)
-        fs(6, 0, 4)
+        abs_(31)
+        fs(6, 0, 2)
         st0(6, 0, 4)
         ks(6, 0, 8)
+        fs(6, 2, 2)
         cc(14, "G")
-        st1(5, 0, 4)
-        abv(31)
-        mx(7, 0, 2)
         cc(15, "G")
-        abs_(31)
+        st1(5, 0, 4)
+        mx(7, 0, 2)
         mx(7, 2, 2)
         ks(6, 8, 16)
         st0(7, 0, 2)

from contextlib import ExitStack

import concourse.mybir as mybir
from concourse.masks import make_identity

F32 = mybir.dt.float32
BF16 = mybir.dt.bfloat16
U32 = mybir.dt.uint32
U8 = mybir.dt.uint8
I32 = mybir.dt.int32
FP8 = mybir.dt.float8_e4m3fn
FP8X4 = mybir.dt.float8_e4m3fn_x4
ALU = mybir.AluOpType
ACT = mybir.ActivationFunctionType
AX = mybir.AxisListType

FLOPS = 2 * 1024 * 2048 * 2048

P = 128
NB, NI, NG, NH = 2, 4, 4, 16
D, NOPE, HALF = 128, 32, 48
ROPE = 2 * HALF
W_CHUNKS = ((0, 256), (256, 256), (512, 512), (1024, 512), (1536, 512))
TWO_PI = 6.283185307179586
RHO = 10000.0 ** (-1.0 / 48.0)
NACC = 6
GROPE = (21, 25, 29)
RC_LATER = (3, 4, 5,)
MERGE_FROM = 6
SPLIT_TO = 0


def tile_mla_pb_kernel(tc, x, Wq, out_0, out_1):
    nc = tc.nc
    with ExitStack() as ctx:
        pool = ctx.enter_context(tc.tile_pool(name="sb", bufs=1))
        psum = ctx.enter_context(tc.psum_pool(name="ps", bufs=1))
        ctx.enter_context(tc.manual_schedule())

        x_codes = pool.tile([P, NB, NI, NG * P], U32, name="x_codes", align_bytes=64)
        x_scales = pool.tile([P, NB, NI, NG * P], U8, name="x_scales", align_bytes=64)
        ws_codes = pool.tile([P, 2, NG, 256], U32, name="ws_codes", align_bytes=64)
        ws_scales = pool.tile([P, 2, NG, 256], U8, name="ws_scales", align_bytes=64)
        wb_codes = pool.tile([P, 3, NG, 512], U32, name="wb_codes", align_bytes=64)
        wb_scales = pool.tile([P, 3, NG, 512], U8, name="wb_scales", align_bytes=64)

        x_raw = {}
        w_raw = {}

        def load_x(b, i):
            t = pool.tile([P, 2048], BF16, name="x_raw%d" % i)
            nc.sync.dma_start(out=t[:], in_=x[b].rearrange("(p i) k -> p i k", i=NI)[:, i, :])
            x_raw[(b, i)] = t

        def load_w(c, g):
            c0, width = W_CHUNKS[c]
            t = pool.tile([P, 4, width], BF16, name="w_raw%d_%d" % (2 if c == 4 else c, g))
            nc.sync.dma_start(out=t[:], in_=Wq[512 * g:512 * (g + 1), c0:c0 + width].rearrange("(p j) w -> p j w", j=4))
            w_raw[(c, g)] = t

        load_x(0, 0)
        load_x(0, 1)
        for g in range(NG):
            load_w(0, g)
        load_x(0, 2)
        load_x(0, 3)
        for g in range(NG):
            load_w(1, g)

        warm = pool.tile([P, 1], F32, name="warm")
        nc.vector.memset(warm[:], 0.0)
        nc.scalar.activation(out=warm[:], in_=warm[:], func=ACT.Sin)
        pos_i = pool.tile([P, NI], I32, name="pos_i")
        nc.gpsimd.iota(pos_i[:], pattern=[[1, NI]], base=0, channel_multiplier=NI)
        ident = pool.tile([P, P], F32, name="ident")
        make_identity(nc, ident[:])
        zero = pool.tile([P, 1], F32, name="zero")
        nc.vector.memset(zero[:], 0.0)
        pos_f = pool.tile([P, NI], F32, name="pos_f")
        nc.vector.tensor_copy(out=pos_f[:], in_=pos_i[:])
        turns = pool.tile([P, 2, NI, HALF], F32, name="turns")
        nc.vector.tensor_scalar(out=turns[:, 0, :, 0:1], in0=pos_f[:].unsqueeze(2), scalar1=1.0 / TWO_PI, scalar2=None,
                                op0=ALU.mult)
        for w in (1, 2, 4, 8, 16, 32):
            n = min(w, HALF - w)
            nc.vector.tensor_scalar(out=turns[:, 0, :, w:w + n], in0=turns[:, 0, :, 0:n], scalar1=RHO ** w, scalar2=None,
                                    op0=ALU.mult)
        nc.vector.tensor_scalar(out=turns[:, 1], in0=turns[:, 0], scalar1=0.25, scalar2=None, op0=ALU.add)
        whole_i = pool.tile([P, 2, NI, HALF], I32, name="whole_i")
        nc.vector.tensor_copy(out=whole_i[:], in_=turns[:])
        whole_f = pool.tile([P, 2, NI, HALF], F32, name="whole_f")
        nc.vector.tensor_copy(out=whole_f[:], in_=whole_i[:])
        frac = pool.tile([P, 2, NI, HALF], F32, name="frac")
        nc.vector.tensor_tensor(out=frac[:], in0=turns[:], in1=whole_f[:], op=ALU.subtract)
        nfrac = pool.tile([P, 2, NI, HALF], F32, name="nfrac")
        fl = "p k i j -> p (k i j)"
        nc.vector.scalar_tensor_tensor(out=nfrac[:].rearrange(fl), in0=frac[:].rearrange(fl), scalar=0.5,
                                       in1=frac[:].rearrange(fl), op0=ALU.is_gt, op1=ALU.subtract)
        tab = pool.tile([P, 2, 2, 2, 2, ROPE], F32, name="tab")

        def sin_tables():
            for e in range(2):
                for h2 in range(2):
                    nc.scalar.activation(out=tab[:, :, 0, :, h2, HALF * e:HALF * (e + 1)],
                                         in_=nfrac[:, 1].rearrange("p (k i) j -> p k i j", k=2), func=ACT.Sin, scale=-TWO_PI)
                    nc.scalar.activation(out=tab[:, :, 1, :, h2, HALF * e:HALF * (e + 1)],
                                         in_=nfrac[:, 0].rearrange("p (k i) j -> p k i j", k=2), func=ACT.Sin,
                                         scale=(-TWO_PI if e == 0 else TWO_PI))

        xt_banks = {}
        x_grp = {}
        w_grp = {}
        acc = {}
        rope = {}
        o_tiles = {}
        o8_tiles = {}
        stats = {}
        q_sb = {}

        def copy_on(eng, out, in_):
            if eng == "V":
                nc.vector.tensor_copy(out=out, in_=in_)
            elif eng == "S":
                nc.scalar.copy(out=out, in_=in_)
            else:
                nc.gpsimd.tensor_scalar(out=out, in0=in_, scalar1=1.0, scalar2=0.0, op0=ALU.mult, op1=ALU.add)

        def xtb(b, i, gp):
            words = x_raw[(b, i)][:].bitcast(F32)
            bank = psum.tile([P, 2, 2, P], F32, name=("xt%d" % gp) if i % 2 == 0 else ("acc%d" % (4 + gp)))
            for gg in range(2):
                g = 2 * gp + gg
                for u in range(2):
                    nc.tensor.transpose(out=bank[:, gg, u, :], in_=words[:, 256 * g + u:256 * (g + 1):2],
                                        identity=ident[:])
            xt_banks[(b, i, gp)] = bank

        def xc(b, i, gp, eng):
            if (b, i // 2) not in x_grp:
                x_grp[(b, i // 2)] = pool.tile([P, 2, NG, P, 4], BF16, name="x_grp%d" % (i // 2), align_bytes=64)
            dst = x_grp[(b, i // 2)][:, i % 2, 2 * gp:2 * gp + 2, :, :].bitcast(F32)
            copy_on(eng, dst, xt_banks[(b, i, gp)][:].rearrange("p g u r -> p g r u"))

        def xq(b, k):
            nc.vector.quantize_mx(out=x_codes[:, b, 2 * k:2 * k + 2, :].rearrange("p i w -> p (i w)").bitcast(FP8X4),
                                  scales=x_scales[:, b, 2 * k:2 * k + 2, :].rearrange("p i w -> p (i w)"),
                                  in_=x_grp[(b, k)][:].rearrange("p i g r t -> p (i g r t)"))

        def wi(c, g, part, eng):
            width = W_CHUNKS[c][1]
            if (c, g // 2) not in w_grp:
                w_grp[(c, g // 2)] = pool.tile([P, 2, width, 4], BF16, name="w_grp%d_%d" % (width, g // 2), align_bytes=64)
            dst = w_grp[(c, g // 2)][:, g % 2].rearrange("p (h d) t -> p h d t", d=D)
            src = w_raw[(c, g)][:].rearrange("p t (h d) -> p h d t", d=D)
            if part == 0:
                copy_on(eng, dst[:, :, 0:NOPE, :], src[:, :, 0:NOPE, :])
            else:
                e = part - 1
                copy_on(eng, dst[:, :, NOPE + HALF * e:NOPE + HALF * (e + 1), :], src[:, :, NOPE + e:D:2, :])

        def wq(c, gq):
            codes, scales = (ws_codes[:, c], ws_scales[:, c]) if c < 2 else (wb_codes[:, c - 2], wb_scales[:, c - 2])
            nc.vector.quantize_mx(out=codes[:, 2 * gq:2 * gq + 2, :].rearrange("p g w -> p (g w)").bitcast(FP8X4),
                                  scales=scales[:, 2 * gq:2 * gq + 2, :].rearrange("p g w -> p (g w)"),
                                  in_=w_grp[(c, gq)][:].rearrange("p g w t -> p (g w t)"))

        def pair_of(m):
            return m // 4, (m // 2) % 2, m % 2

        def mm(n):
            nt, b, hp = pair_of(n // 2)
            a = psum.tile([P, 2, 2 * D], F32, name="acc%d" % (n % NACC))
            for i2 in range(2):
                i = 2 * (n % 2) + i2
                for g in range(NG):
                    if nt == 0:
                        rhs, rhs_scale = ws_codes[:, hp, g, :], ws_scales[:, hp, g, :]
                    else:
                        rhs = wb_codes[:, nt - 1, g, 256 * hp:256 * (hp + 1)]
                        rhs_scale = wb_scales[:, nt - 1, g, 256 * hp:256 * (hp + 1)]
                    nc.tensor.matmul_mx(out=a[:, i2, :], lhsT=x_codes[:, b, i, P * g:P * (g + 1)].bitcast(FP8X4),
                                        lhsT_scale=x_scales[:, b, i, P * g:P * (g + 1)], rhs=rhs.bitcast(FP8X4),
                                        rhs_scale=rhs_scale, start=(g == 0), stop=(g == NG - 1))
            acc[n] = a

        def o32_of(nt, b):
            if (nt, b) not in o_tiles:
                o_tiles[(nt, b)] = pool.tile([P, 4, NI, D], F32, name="o32_%d" % ((2 * nt + b) % 3))
            return o_tiles[(nt, b)]

        def o8_of(nt, b):
            if (nt, b) not in o8_tiles:
                o8_tiles[(nt, b)] = pool.tile([P, 4, NI, D], FP8, name="o8_%d" % ((2 * nt + b) % 3))
            return o8_tiles[(nt, b)]

        def abs_(n):
            m, k = n // 2, n % 2
            nt, b, hp = pair_of(m)
            nc.scalar.copy(out=o32_of(nt, b)[:, 2 * hp:2 * hp + 2, 2 * k:2 * k + 2, 0:NOPE],
                           in_=acc[n][:].rearrange("p i (h d) -> p h i d", h=2)[:, :, :, 0:NOPE])

        def abv(n):
            m, k = n // 2, n % 2
            if m not in rope:
                rope[m] = pool.tile([P, 2, 2, 4, ROPE], F32, name="rope%d" % (m % 3))
            q = acc[n][:].rearrange("p i (h d) -> p (i h) d", h=2)[:, :, NOPE:D]
            nc.vector.tensor_tensor(out=rope[m][:, :, k], in0=tab[:, k].rearrange("p s i h c -> p s (i h) c"),
                                    in1=q.unsqueeze(1).to_broadcast([P, 2, 4, ROPE]), op=ALU.mult)

        def abq(n):
            q = acc[n][:].rearrange("p i (h d) -> p (i h) d", h=2)[:, :, NOPE:D]
            q_sb[n] = pool.tile([P, 4, ROPE], F32, name="q_sb%d" % ((n // 4) % 2))
            nc.scalar.copy(out=q_sb[n][:], in_=q)

        def abg(n):
            m, k = n // 2, n % 2
            if m not in rope:
                rope[m] = pool.tile([P, 2, 2, 4, ROPE], F32, name="rope%d" % (m % 3))
            nc.gpsimd.tensor_tensor(out=rope[m][:, :, k], in0=tab[:, k].rearrange("p s i h c -> p s (i h) c"),
                                    in1=q_sb[n][:].unsqueeze(1).to_broadcast([P, 2, 4, ROPE]), op=ALU.mult)

        def ab(n):
            if n in GROPE:
                abq(n)
                abg(n)
            else:
                abv(n)
            abs_(n)

        def cc(m, eng):
            nt, b, hp = pair_of(m)
            o32 = o32_of(nt, b)
            e = nc.gpsimd if eng == "G" else nc.vector
            if m >= MERGE_FROM:
                e.tensor_tensor(out=o32[:, 2 * hp:2 * hp + 2, :, NOPE:D].rearrange("p h r (f j) -> p r h f j", f=2),
                                in0=rope[m][:, 0].rearrange("p k (i h) (f j) -> p (k i) h f j", h=2, f=2),
                                in1=rope[m][:, 1].rearrange("p k (i h) (f j) -> p (k i) h f j", h=2, f=2)[:, :, :, ::-1, :],
                                op=ALU.add)
                return
            for f in range(2):
                for h in (range(2) if m < SPLIT_TO else (None,)):
                    hs = slice(0, 2) if h is None else slice(h, h + 1)
                    e.tensor_tensor(out=o32[:, 2 * hp:2 * hp + 2, :, NOPE + HALF * f:NOPE + HALF * (f + 1)][:, hs],
                                    in0=rope[m][:, 0, :, :, HALF * f:HALF * (f + 1)].rearrange("p k (i h) j -> p h (k i) j", h=2)[:, hs],
                                    in1=rope[m][:, 1, :, :, HALF * (1 - f):HALF * (2 - f)].rearrange("p k (i h) j -> p h (k i) j", h=2)[:, hs],
                                    op=ALU.add)

        def mx(u, h0, nh):
            nt, b = u // 2, u % 2
            o32 = o32_of(nt, b)
            if u not in stats:
                stats[u] = (pool.tile([P, 16], F32, name="amax%d" % (u % 3)), pool.tile([P, 16], F32, name="rcp%d" % (u % 3)),
                            pool.tile([P, 16], F32, name="fac%d" % (u % 3)))
            cols = slice(4 * h0, 4 * (h0 + nh))
            nc.vector.tensor_reduce(out=stats[u][0][:, cols], in_=o32[:, h0:h0 + nh].rearrange("p h i d -> p (h i) d"),
                                    axis=AX.X, op=ALU.max, apply_absolute_value=True)
            if u not in RC_LATER:
                nc.vector.reciprocal(out=stats[u][1][:, cols], in_=stats[u][0][:, cols])

        def rc(u, h0, nh):
            cols = slice(4 * h0, 4 * (h0 + nh))
            nc.vector.reciprocal(out=stats[u][1][:, cols], in_=stats[u][0][:, cols])

        def fs(u, h0, nh):
            cols = slice(4 * h0, 4 * (h0 + nh))
            nc.scalar.activation(out=stats[u][2][:, cols], in_=stats[u][1][:, cols], func=ACT.Copy, scale=448.0)

        def fv(u, h0, nh):
            cols = slice(4 * h0, 4 * (h0 + nh))
            nc.vector.tensor_scalar(out=stats[u][2][:, cols], in0=stats[u][1][:, cols], scalar1=448.0, scalar2=None,
                                    op0=ALU.mult)

        def ks(u, r0, r1):
            nt, b = u // 2, u % 2
            o32, o8 = o32_of(nt, b), o8_of(nt, b)
            for r in range(r0, r1):
                nc.scalar.activation(out=o8[:, r // 4, r % 4, :], in_=o32[:, r // 4, r % 4, :], func=ACT.Identity,
                                     scale=stats[u][2][:, r:r + 1], bias=zero[:, 0:1], saturate=False)

        def kv(u, r0, r1):
            nt, b = u // 2, u % 2
            o32, o8 = o32_of(nt, b), o8_of(nt, b)
            for r in range(r0, r1):
                nc.vector.tensor_scalar(out=o8[:, r // 4, r % 4, :], in0=o32[:, r // 4, r % 4, :],
                                        scalar1=stats[u][2][:, r:r + 1], scalar2=None, op0=ALU.mult, saturate=False)

        def st0(u, h0, nh):
            nt, b = u // 2, u % 2
            nc.sync.dma_start(out=out_0[b, 4 * nt + h0:4 * nt + h0 + nh].rearrange("h (p i) d -> p h (i d)", i=NI),
                              in_=o32_of(nt, b)[:, h0:h0 + nh].rearrange("p h i d -> p h (i d)"))

        def st1(u, h0, nh):
            nt, b = u // 2, u % 2
            nc.sync.dma_start(out=out_1[b, 4 * nt + h0:4 * nt + h0 + nh].rearrange("h (p i) d -> p h (i d)", i=NI),
                              in_=o8_of(nt, b)[:, h0:h0 + nh].bitcast(U8).rearrange("p h i d -> p h (i d)"))

        wi(0, 0, 2, "G")
        xtb(0, 0, 0)
        xc(0, 0, 0, "S")
        xtb(0, 0, 1)
        xc(0, 0, 1, "S")
        xtb(0, 1, 0)
        xc(0, 1, 0, "V")
        xtb(0, 1, 1)
        xc(0, 1, 1, "V")
        wi(0, 1, 2, "V")
        wi(0, 2, 2, "V")
        wi(0, 2, 1, "V")
        wi(0, 2, 0, "S")
        xtb(0, 2, 1)
        load_x(1, 0)
        wi(0, 1, 0, "S")
        xtb(0, 2, 0)
        wi(0, 1, 1, "G")
        wi(0, 0, 1, "S")
        load_x(1, 1)
        load_w(2, 0)
        wi(0, 0, 0, "S")
        wi(0, 3, 2, "S")
        wi(0, 3, 0, "S")
        xc(0, 2, 1, "S")
        sin_tables()
        wi(0, 3, 1, "V")
        xq(0, 0)
        wq(0, 0)
        xc(0, 2, 0, "V")
        wq(0, 1)
        wi(1, 0, 0, "S")
        xtb(0, 3, 1)
        xtb(0, 3, 0)
        wi(1, 1, 1, "S")
        wi(1, 0, 2, "V")
        wi(1, 2, 0, "S")
        wi(1, 3, 1, "S")
        load_x(1, 2)
        wi(1, 2, 2, "V")
        mm(0)
        xc(0, 3, 0, "V")
        xtb(1, 0, 0)
        wi(1, 0, 1, "S")
        xc(0, 3, 1, "V")
        wi(1, 1, 2, "G")
        wi(1, 1, 0, "S")
        xtb(1, 0, 1)
        xc(1, 0, 0, "S")
        xc(1, 0, 1, "S")
        abv(0)
        load_w(2, 1)
        load_x(1, 3)
        wi(1, 3, 2, "S")
        load_w(2, 2)
        wi(1, 2, 1, "G")
        xtb(1, 1, 0)
        xc(1, 1, 0, "S")
        xtb(1, 1, 1)
        load_w(2, 3)
        wi(1, 3, 0, "V")
        xc(1, 1, 1, "S")
        load_w(3, 0)
        wq(1, 0)
        wi(2, 0, 0, "S")
        xq(0, 1)
        wi(2, 0, 1, "V")
        wi(2, 0, 2, "V")
        xtb(1, 2, 0)
        xtb(1, 2, 1)
        wq(1, 1)
        wi(2, 1, 2, "S")
        xc(1, 2, 1, "S")
        xq(1, 0)
        mm(2)
        xc(1, 2, 0, "S")
        mm(1)
        wi(2, 1, 1, "V")
        wi(2, 2, 0, "S")
        wi(2, 1, 0, "V")
        xtb(1, 3, 1)
        load_w(3, 1)
        wi(2, 2, 1, "S")
        xtb(1, 3, 0)
        wq(2, 0)
        abv(1)
        wi(2, 2, 2, "G")
        load_w(4, 1)
        load_w(3, 2)
        xc(1, 3, 0, "S")
        xc(1, 3, 1, "S")
        wi(2, 3, 1, "S")
        xq(1, 1)
        mm(4)
        mm(5)
        abs_(1)
        abs_(0)
        load_w(3, 3)
        cc(0, "G")
        abv(2)
        wi(2, 3, 0, "S")
        wi(2, 3, 2, "S")
        wi(3, 0, 1, "S")
        mm(3)
        abv(4)
        abs_(2)
        wq(2, 1)
        wi(3, 0, 2, "S")
        wi(3, 1, 2, "G")
        mm(7)
        abv(3)
        wi(3, 1, 0, "S")
        mm(6)
        abs_(3)
        cc(1, "G")
        wi(3, 1, 1, "S")
        abv(5)
        wi(3, 2, 0, "S")
        wi(3, 0, 0, "S")
        wi(3, 2, 1, "S")
        mm(9)
        abs_(4)
        abs_(5)
        abv(6)
        mm(8)
        wi(3, 3, 0, "S")
        wi(3, 3, 2, "S")
        abv(7)
        abs_(7)
        mm(11)
        mm(10)
        wi(3, 3, 1, "S")
        wi(3, 2, 2, "S")
        abv(9)
        load_w(4, 0)
        abv(8)
        load_w(4, 2)
        cc(2, "G")
        abs_(6)
        mm(12)
        wq(3, 0)
        abs_(9)
        cc(4, "G")
        abv(11)
        wi(4, 1, 0, "S")
        mx(0, 0, 4)
        abv(10)
        st0(0, 0, 4)
        cc(3, "G")
        wi(4, 0, 0, "S")
        wq(3, 1)
        cc(5, "G")
        wi(4, 0, 1, "S")
        abs_(8)
        wi(4, 1, 1, "G")
        wi(4, 0, 2, "S")
        mm(14)
        mm(15)
        wi(4, 1, 2, "S")
        abs_(11)
        load_w(4, 3)
        mx(1, 0, 4)
        abv(15)
        abv(14)
        wi(4, 2, 2, "S")
        fs(0, 0, 4)
        st0(1, 0, 4)
        wi(4, 2, 1, "G")
        mm(17)
        fs(1, 0, 4)
        wi(4, 3, 1, "S")
        abs_(10)
        wi(4, 2, 0, "S")
        st0(2, 0, 4)
        mm(13)
        ks(0, 8, 16)
        wi(4, 3, 0, "S")
        abv(13)
        mm(16)
        wi(4, 3, 2, "G")
        ks(0, 0, 8)
        abv(12)
        wq(4, 0)
        wq(4, 1)
        abs_(12)
        abs_(14)
        mm(18)
        abv(16)
        ks(1, 8, 16)
        cc(7, "G")
        abv(17)
        abs_(15)
        abs_(13)
        ks(1, 0, 8)
        mm(21)
        mx(2, 0, 4)
        abq(21)
        mm(20)
        abs_(16)
        abs_(17)
        fs(2, 0, 4)
        cc(6, "G")
        abv(18)
        abv(20)
        st1(0, 0, 4)
        mx(3, 0, 4)
        mm(22)
        ks(2, 8, 16)
        ks(2, 0, 8)
        st0(3, 0, 4)
        abg(21)
        abs_(18)
        mm(23)
        mm(19)
        abs_(21)
        abs_(20)
        cc(8, "G")
        abv(19)
        rc(3, 0, 4)
        fs(3, 0, 4)
        ks(3, 8, 16)
        abs_(19)
        mm(27)
        abv(23)
        cc(10, "G")
        ks(3, 0, 8)
        abv(22)
        cc(9, "G")
        abv(27)
        mm(24)
        st1(1, 0, 4)
        mm(26)
        st1(2, 0, 4)
        mm(25)
        abs_(22)
        abq(25)
        cc(11, "G")
        mx(4, 0, 4)
        abg(25)
        abs_(27)
        abv(24)
        rc(4, 0, 4)
        abs_(25)
        abs_(23)
        fs(4, 0, 4)
        abv(26)
        mm(29)
        mx(5, 0, 4)
        ks(4, 0, 8)
        abs_(24)
        abq(29)
        mm(28)
        mm(30)
        cc(12, "G")
        abs_(26)
        st1(3, 0, 4)
        st0(4, 0, 4)
        ks(4, 8, 16)
        abv(28)
        rc(5, 0, 4)
        st0(5, 0, 4)
        mm(31)
        cc(13, "G")
        abv(30)
        abv(31)
        abs_(29)
        fs(5, 0, 4)
        st1(4, 0, 4)
        abg(29)
        ks(5, 0, 8)
        abs_(30)
        ks(5, 8, 16)
        mx(6, 0, 2)
        mx(6, 2, 2)
        abs_(28)
        abs_(31)
        fs(6, 0, 2)
        st0(6, 0, 4)
        ks(6, 0, 8)
        fs(6, 2, 2)
        cc(14, "G")
        cc(15, "G")
        st1(5, 0, 4)
        mx(7, 0, 2)
        mx(7, 2, 2)
        ks(6, 8, 16)
        st0(7, 0, 2)
        fv(7, 2, 2)
        fs(7, 0, 2)
        ks(7, 0, 8)
        st0(7, 2, 2)
        st1(6, 0, 4)
        ks(7, 13, 16)
        kv(7, 8, 13)
        st1(7, 0, 2)
        st1(7, 2, 2)
